import numpy as np
import ml_dtypes


def mxq(x, axis, fmt="e4m3"):
    dtype, down = {"e4m3": (ml_dtypes.float8_e4m3fn, 7), "e5m2": (ml_dtypes.float8_e5m2, 14)}[fmt]
    v = np.moveaxis(np.asarray(x, np.float32).astype(ml_dtypes.bfloat16).astype(np.float64), axis, -1)
    blocks = v.reshape(v.shape[:-1] + (-1, 32))
    amax = np.abs(blocks).max(-1, keepdims=True)
    byte = np.maximum(np.where(amax > 0, np.frexp(amax)[1] - 1 + 127, 0) - down, 1)
    scale = np.exp2(byte - 127.0)
    codes = (blocks / scale).astype(np.float32).astype(dtype).astype(np.float64)
    return np.moveaxis((codes * scale).reshape(v.shape), -1, axis)


WIDE = False


def mx_kscale(k):
    if not WIDE:
        return np.ones(k)
    levels = np.array([10, -10, 5, -5, 0])
    if k % 512:
        return np.exp2(np.random.permutation(np.resize(levels, k // 32))).repeat(32)
    a = np.empty((k // 512, 16))
    for p in range(k // 512):
        a[p, :8] = np.random.permutation(np.resize(levels, 8))
        for g in range(8):
            far = levels[np.abs(levels - a[p, g]) >= 10]
            a[p, g + 8] = far[np.random.randint(len(far))]
    return np.exp2(a.ravel()).repeat(32)


BF16 = ml_dtypes.bfloat16


def bf(x):
    return np.asarray(x, np.float32).astype(BF16)


def f64(x):
    return np.asarray(x).astype(np.float64)


B, C, HH, WW = 1, 1024, 8, 16
N = HH * WW


def setup_inputs():
    s, t = mx_kscale(C), mx_kscale(C)
    return {"x": bf(np.random.standard_normal((B, C, HH, WW)) * s[None, :, None, None]),
            "Wq": bf(np.random.standard_normal((C, C)) * 1.4 / np.sqrt(C) * t[:, None] / s[None, :]),
            "bq": bf(np.random.standard_normal(C) * 0.2 * t),
            "k": bf(np.random.standard_normal((B, N, C)) * 1.4 / t)}


def reference(x, Wq, bq, k):
    xt = f64(x).reshape(B, C, N)
    q = (mxq(xt, 1, "e4m3").transpose(0, 2, 1) @ mxq(f64(Wq), 1, "e4m3").T) + f64(bq)
    scores = mxq(q / np.sqrt(C), 2, "e4m3") @ mxq(f64(k), 2, "e4m3").transpose(0, 2, 1)
    e = np.exp(scores - scores.max(-1, keepdims=True))
    return e / e.sum(-1, keepdims=True)

@@ -1,0 +1,206 @@
+from contextlib import ExitStack
+
+import concourse.mybir as mybir
+from concourse.masks import make_identity
+
+F32 = mybir.dt.float32
+BF16 = mybir.dt.bfloat16
+U32 = mybir.dt.uint32
+U8 = mybir.dt.uint8
+FP8X4 = mybir.dt.float8_e4m3fn_x4
+ACT = mybir.ActivationFunctionType
+ALU = mybir.AluOpType
+AXIS = mybir.AxisListType
+
+P = 128
+TOKENS = 128
+CHANNELS = 1024
+PACK = 4
+K_PASS = P * PACK
+PASSES = CHANNELS // K_PASS
+PAIR = 2
+HALVES = PACK // PAIR
+O_TILES = CHANNELS // P
+TILES_PER_PASS = O_TILES // PASSES
+ROUND_TILES = 4
+ROUNDS = O_TILES // ROUND_TILES
+ROUNDS_PER_PASS = TILES_PER_PASS // ROUND_TILES
+
+FLOPS = 2 * TOKENS * CHANNELS * CHANNELS + 2 * TOKENS * TOKENS * CHANNELS
+
+
+def tile_visionattention_pa_s_kernel(tc, x, Wq, bq, k, out):
+    nc = tc.nc
+    with ExitStack() as ctx:
+        ctx.enter_context(tc.manual_schedule())
+        keep = ctx.enter_context(tc.tile_pool(name="keep", bufs=1))
+        per_tile = ctx.enter_context(tc.tile_pool(name="per_tile", bufs=O_TILES))
+        per_pass = ctx.enter_context(tc.tile_pool(name="per_pass", bufs=PASSES))
+        psum_t = ctx.enter_context(tc.psum_pool(name="psum_t", bufs=4))
+        psum_q = ctx.enter_context(tc.psum_pool(name="psum_q", bufs=PASSES))
+        psum_one = ctx.enter_context(tc.psum_pool(name="psum_one", bufs=1))
+
+        bq_rows = keep.tile([P, K_PASS], BF16)
+        nc.vector.memset(bq_rows[:], 0.0)
+        zero_col = keep.tile([P, 1], F32)
+        nc.vector.memset(zero_col[:], 0.0)
+        nc.scalar.dma_start(
+            out=bq_rows[0:PASSES, :], in_=bq.rearrange("(g w) -> g w", g=PASSES)
+        )
+
+        wq_sb = keep.tile([P, O_TILES * CHANNELS], BF16)
+        wq_tiles = wq_sb[:].rearrange("p (j c) -> p j c", j=O_TILES)
+        wq_rows = Wq.rearrange("(g r t) c -> r g t c", r=P, t=PACK)
+        x_sb = keep.tile([P, CHANNELS], BF16)
+        k_sb = keep.tile([P, CHANNELS], BF16)
+        for j in range(O_TILES):
+            if j == ROUND_TILES:
+                nc.sync.dma_start(
+                    out=x_sb[:].rearrange("p (g tn) -> p g tn", g=PASSES),
+                    in_=x.rearrange("b c h w -> c (b h w)").rearrange(
+                        "(g p t) n -> p g (t n)", p=P, t=PACK
+                    ),
+                )
+            nc.sync.dma_start(out=wq_tiles[:, j, :], in_=wq_rows[:, j // PACK, j % PACK, :])
+        nc.sync.dma_start(out=k_sb[:], in_=k.rearrange("b m c -> (b m) c"))
+        wq_words = wq_sb[:].bitcast(F32).rearrange("p (j w) -> p j w", j=O_TILES)
+        k_words = k_sb[:].bitcast(F32)
+
+        ident = keep.tile([P, P], F32)
+        make_identity(nc, ident[:])
+
+        warm = keep.tile([P, 1], F32)
+        nc.scalar.activation(out=warm[:], in_=zero_col[:], func=ACT.Exp)
+
+        x_grouped = keep.tile([P, PASSES * TOKENS * PACK], BF16, align_bytes=64)
+        nc.vector.tensor_copy(
+            out=x_grouped[:].rearrange("p (g n t) -> p g n t", g=PASSES, t=PACK),
+            in_=x_sb[:].rearrange("p (g t n) -> p g n t", g=PASSES, t=PACK),
+        )
+        x_codes = keep.tile([P, PASSES * TOKENS], U32, align_bytes=64)
+        x_scales = keep.tile([P, PASSES * TOKENS], U8, align_bytes=64)
+        nc.vector.quantize_mx(out=x_codes[:].bitcast(FP8X4), scales=x_scales[:], in_=x_grouped[:])
+
+        def transpose_rows(words):
+            bank = psum_t.tile([P, PASSES, HALVES, P], F32)
+            for g in range(PASSES):
+                for u in range(HALVES):
+                    group = slice(g * HALVES * P + u, (g + 1) * HALVES * P, HALVES)
+                    nc.tensor.transpose(bank[:, g, u, :], words[:, group], ident[:])
+            return bank
+
+        def empty_bank(bank):
+            grouped = per_tile.tile([P, PASSES * P * PACK], BF16, align_bytes=64, bufs=O_TILES + 1)
+            nc.scalar.copy(
+                out=grouped[:].bitcast(F32).rearrange("p (g r u) -> p g r u", g=PASSES, u=HALVES),
+                in_=bank[:].rearrange("p g u r -> p g r u"),
+            )
+            return grouped
+
+        def quantise_rows(grouped):
+            codes = per_tile.tile([P, PASSES * P], U32, align_bytes=64, bufs=O_TILES + 1)
+            scales = per_tile.tile([P, PASSES * P], U8, align_bytes=64, bufs=O_TILES + 1)
+            nc.vector.quantize_mx(out=codes[:].bitcast(FP8X4), scales=scales[:], in_=grouped[:])
+            return codes, scales
+
+        qT = []
+        for g in range(PASSES):
+            q_bank = psum_q.tile([P, TILES_PER_PASS, TOKENS], F32)
+            qT.append(q_bank)
+
+        def project_tile(j, codes, scales):
+            for g in range(PASSES):
+                cols = slice(g * P, (g + 1) * P)
+                nc.tensor.matmul_mx(
+                    out=qT[j // TILES_PER_PASS][:, j % TILES_PER_PASS, :],
+                    lhsT=codes[:, cols].bitcast(FP8X4),
+                    lhsT_scale=scales[:, cols],
+                    rhs=x_codes[:, cols].bitcast(FP8X4),
+                    rhs_scale=x_scales[:, cols],
+                    start=(g == 0),
+                    stop=(g == PASSES - 1),
+                )
+
+        bias = keep.tile([P, O_TILES], F32)
+
+        def finish_q_pass(g):
+            grouped = per_pass.tile([P, TOKENS * PACK], BF16, align_bytes=64)
+            nc.vector.scalar_tensor_tensor(
+                out=grouped[:].rearrange("p (n t) -> p n t", t=PACK),
+                in0=qT[g][:].rearrange("p t n -> p n t"),
+                scalar=1.0 / 32.0,
+                in1=bias[:, g * PACK : (g + 1) * PACK].unsqueeze(1).to_broadcast([P, TOKENS, PACK]),
+                op0=ALU.mult,
+                op1=ALU.add,
+            )
+            codes = per_pass.tile([P, TOKENS], U32, align_bytes=64)
+            scales = per_pass.tile([P, TOKENS], U8, align_bytes=64)
+            nc.vector.quantize_mx(out=codes[:].bitcast(FP8X4), scales=scales[:], in_=grouped[:])
+            return codes, scales
+
+        def tiles_of_round(a):
+            if 0 <= a < ROUNDS:
+                return range(a * ROUND_TILES, (a + 1) * ROUND_TILES)
+            return range(0)
+
+        banks = {}
+        grouped_rows = {}
+        quantised = {}
+        q_quantised = {}
+        for a in range(ROUNDS + 2):
+            for j in tiles_of_round(a):
+                banks[j] = transpose_rows(wq_words[:, j, :])
+            if a == 0:
+                bqT = psum_one.tile([P, HALVES, P], F32, tag="small")
+                for u in range(HALVES):
+                    nc.tensor.transpose(bqT[:, u, :], bq_rows[:].bitcast(F32)[:, u::HALVES], ident[:])
+                nc.vector.tensor_scalar(
+                    out=bias[:].rearrange("p (g u e) -> p g u e", g=PASSES, u=HALVES),
+                    in0=bqT[:, :, 0:PASSES].bitcast(BF16).rearrange("p u (g e) -> p g u e", e=PAIR),
+                    scalar1=1.0 / 32.0,
+                    scalar2=None,
+                    op0=ALU.mult,
+                )
+            if a == ROUNDS:
+                banks["k"] = transpose_rows(k_words)
+            for j in tiles_of_round(a - 1):
+                quantised[j] = quantise_rows(grouped_rows[j])
+            if a == ROUNDS + 1:
+                quantised["k"] = quantise_rows(grouped_rows["k"])
+            if a >= 2 and (a - 1) % ROUNDS_PER_PASS == 0:
+                g = (a - 1) // ROUNDS_PER_PASS - 1
+                q_quantised[g] = finish_q_pass(g)
+            for j in tiles_of_round(a):
+                grouped_rows[j] = empty_bank(banks[j])
+            if a == ROUNDS:
+                grouped_rows["k"] = empty_bank(banks["k"])
+            for j in tiles_of_round(a - 1):
+                project_tile(j, quantised[j][0], quantised[j][1])
+
+        scores = psum_one.tile([P, TOKENS], F32, tag="small")
+        for g in range(PASSES):
+            cols = slice(g * TOKENS, (g + 1) * TOKENS)
+            nc.tensor.matmul_mx(
+                out=scores[:],
+                lhsT=q_quantised[g][0][:].bitcast(FP8X4),
+                lhsT_scale=q_quantised[g][1][:],
+                rhs=quantised["k"][0][:, cols].bitcast(FP8X4),
+                rhs_scale=quantised["k"][1][:, cols],
+                start=(g == 0),
+                stop=(g == PASSES - 1),
+            )
+
+        neg_max = keep.tile([P, 1], F32)
+        nc.vector.tensor_reduce(out=neg_max[:], in_=scores[:], axis=AXIS.X, op=ALU.max, negate=True)
+        expo = keep.tile([P, TOKENS], F32)
+        row_sum = keep.tile([P, 1], F32)
+        nc.scalar.activation(
+            out=expo[:], in_=scores[:], func=ACT.Exp, bias=neg_max[:], scale=1.0, accum_out=row_sum[:]
+        )
+        inv_sum = keep.tile([P, 1], F32)
+        nc.vector.reciprocal(out=inv_sum[:], in_=row_sum[:])
+        prob = keep.tile([P, TOKENS], F32)
+        nc.vector.tensor_scalar(
+            out=prob[:], in0=expo[:], scalar1=inv_sum[:, 0:1], scalar2=None, op0=ALU.mult
+        )
+        nc.sync.dma_start(out=out.rearrange("b n m -> (b n) m"), in_=prob[:])

@@ -25,6 +25,7 @@ TILES_PER_PASS = O_TILES // PASSES
 ROUND_TILES = 4
 ROUNDS = O_TILES // ROUND_TILES
 ROUNDS_PER_PASS = TILES_PER_PASS // ROUND_TILES
+WARM_COLUMNS = 512
 
 FLOPS = 2 * TOKENS * CHANNELS * CHANNELS + 2 * TOKENS * TOKENS * CHANNELS
 
@@ -41,9 +42,9 @@ def tile_visionattention_pa_s_kernel(tc, x, Wq, bq, k, out):
         psum_one = ctx.enter_context(tc.psum_pool(name="psum_one", bufs=1))
 
         bq_rows = keep.tile([P, K_PASS], BF16)
-        nc.vector.memset(bq_rows[:], 0.0)
         zero_col = keep.tile([P, 1], F32)
         nc.vector.memset(zero_col[:], 0.0)
+        nc.vector.memset(bq_rows[:], 0.0)
         nc.scalar.dma_start(
             out=bq_rows[0:PASSES, :], in_=bq.rearrange("(g w) -> g w", g=PASSES)
         )
@@ -65,6 +66,15 @@ def tile_visionattention_pa_s_kernel(tc, x, Wq, bq, k, out):
         nc.sync.dma_start(out=k_sb[:], in_=k.rearrange("b m c -> (b m) c"))
         wq_words = wq_sb[:].bitcast(F32).rearrange("p (j w) -> p j w", j=O_TILES)
         k_words = k_sb[:].bitcast(F32)
+
+        warm_bank = psum_one.tile([P, WARM_COLUMNS], F32)
+        nc.tensor.matmul(
+            warm_bank[:],
+            lhsT=zero_col[:].to_broadcast([P, P]),
+            rhs=zero_col[:].to_broadcast([P, WARM_COLUMNS]),
+            start=True,
+            stop=True,
+        )
 
         ident = keep.tile([P, P], F32)
         make_identity(nc, ident[:])

@@ -22,9 +22,6 @@ PAIR = 2
 HALVES = PACK // PAIR
 O_TILES = CHANNELS // P
 TILES_PER_PASS = O_TILES // PASSES
-ROUND_TILES = 4
-ROUNDS = O_TILES // ROUND_TILES
-ROUNDS_PER_PASS = TILES_PER_PASS // ROUND_TILES
 WARM_COLUMNS = 512
 
 FLOPS = 2 * TOKENS * CHANNELS * CHANNELS + 2 * TOKENS * TOKENS * CHANNELS
@@ -35,39 +32,47 @@ def tile_visionattention_pa_s_kernel(tc, x, Wq, bq, k, out):
     with ExitStack() as ctx:
         ctx.enter_context(tc.manual_schedule())
         keep = ctx.enter_context(tc.tile_pool(name="keep", bufs=1))
-        per_tile = ctx.enter_context(tc.tile_pool(name="per_tile", bufs=O_TILES))
+        per_tile = ctx.enter_context(tc.tile_pool(name="per_tile", bufs=O_TILES + 1))
         per_pass = ctx.enter_context(tc.tile_pool(name="per_pass", bufs=PASSES))
-        psum_t = ctx.enter_context(tc.psum_pool(name="psum_t", bufs=4))
+        psum_t = ctx.enter_context(tc.psum_pool(name="psum_t", bufs=5))
         psum_q = ctx.enter_context(tc.psum_pool(name="psum_q", bufs=PASSES))
         psum_one = ctx.enter_context(tc.psum_pool(name="psum_one", bufs=1))
 
-        bq_rows = keep.tile([P, K_PASS], BF16)
         zero_col = keep.tile([P, 1], F32)
         nc.vector.memset(zero_col[:], 0.0)
+        bq_rows = keep.tile([P, K_PASS // PAIR], F32)
         nc.vector.memset(bq_rows[:], 0.0)
-        nc.scalar.dma_start(
-            out=bq_rows[0:PASSES, :], in_=bq.rearrange("(g w) -> g w", g=PASSES)
-        )
 
         wq_sb = keep.tile([P, O_TILES * CHANNELS], BF16)
         wq_tiles = wq_sb[:].rearrange("p (j c) -> p j c", j=O_TILES)
         wq_rows = Wq.rearrange("(g r t) c -> r g t c", r=P, t=PACK)
         x_sb = keep.tile([P, CHANNELS], BF16)
         k_sb = keep.tile([P, CHANNELS], BF16)
-        for j in range(O_TILES):
-            if j == ROUND_TILES:
-                nc.sync.dma_start(
-                    out=x_sb[:].rearrange("p (g tn) -> p g tn", g=PASSES),
-                    in_=x.rearrange("b c h w -> c (b h w)").rearrange(
-                        "(g p t) n -> p g (t n)", p=P, t=PACK
-                    ),
-                )
-            nc.sync.dma_start(out=wq_tiles[:, j, :], in_=wq_rows[:, j // PACK, j % PACK, :])
+
+        def load_tiles(first, count):
+            nc.sync.dma_start(
+                out=wq_tiles[:, first : first + count, :],
+                in_=wq_rows[:, first // PACK, first % PACK : first % PACK + count, :],
+            )
+
+        load_tiles(0, 1)
+        nc.sync.dma_start(
+            out=x_sb[:].rearrange("p (g tn) -> p g tn", g=PASSES),
+            in_=x.rearrange("b c h w -> c (b h w)").rearrange("(g p t) n -> p g (t n)", p=P, t=PACK),
+        )
+        nc.scalar.dma_start(
+            out=bq_rows[0:PASSES, :].bitcast(BF16), in_=bq.rearrange("(g w) -> g w", g=PASSES)
+        )
+        load_tiles(1, 2)
+        load_tiles(3, 1)
+        load_tiles(4, 1)
+        load_tiles(5, 2)
+        load_tiles(7, 1)
         nc.sync.dma_start(out=k_sb[:], in_=k.rearrange("b m c -> (b m) c"))
         wq_words = wq_sb[:].bitcast(F32).rearrange("p (j w) -> p j w", j=O_TILES)
         k_words = k_sb[:].bitcast(F32)
 
-        warm_bank = psum_one.tile([P, WARM_COLUMNS], F32)
+        warm_bank = psum_one.tile([P, WARM_COLUMNS], F32, tag="small")
         nc.tensor.matmul(
             warm_bank[:],
             lhsT=zero_col[:].to_broadcast([P, P]),
@@ -82,34 +87,36 @@ def tile_visionattention_pa_s_kernel(tc, x, Wq, bq, k, out):
         warm = keep.tile([P, 1], F32)
         nc.scalar.activation(out=warm[:], in_=zero_col[:], func=ACT.Exp)
 
-        x_grouped = keep.tile([P, PASSES * TOKENS * PACK], BF16, align_bytes=64)
-        nc.vector.tensor_copy(
-            out=x_grouped[:].rearrange("p (g n t) -> p g n t", g=PASSES, t=PACK),
-            in_=x_sb[:].rearrange("p (g t n) -> p g n t", g=PASSES, t=PACK),
-        )
-        x_codes = keep.tile([P, PASSES * TOKENS], U32, align_bytes=64)
-        x_scales = keep.tile([P, PASSES * TOKENS], U8, align_bytes=64)
-        nc.vector.quantize_mx(out=x_codes[:].bitcast(FP8X4), scales=x_scales[:], in_=x_grouped[:])
+        def transpose_pass(words, g, bank):
+            for u in range(HALVES):
+                group = slice(g * HALVES * P + u, (g + 1) * HALVES * P, HALVES)
+                nc.tensor.transpose(bank[:, u, :], words[:, group], ident[:])
 
         def transpose_rows(words):
-            bank = psum_t.tile([P, PASSES, HALVES, P], F32)
+            bank = psum_t.tile([P, PASSES, HALVES, P], F32, tag="bank")
             for g in range(PASSES):
-                for u in range(HALVES):
-                    group = slice(g * HALVES * P + u, (g + 1) * HALVES * P, HALVES)
-                    nc.tensor.transpose(bank[:, g, u, :], words[:, group], ident[:])
+                transpose_pass(words, g, bank[:, g, :, :])
             return bank
 
+        def new_grouped():
+            grouped = per_tile.tile([P, PASSES * P * PACK], BF16, align_bytes=64, tag="grouped")
+            return grouped
+
         def empty_bank(bank):
-            grouped = per_tile.tile([P, PASSES * P * PACK], BF16, align_bytes=64, bufs=O_TILES + 1)
+            grouped = new_grouped()
             nc.scalar.copy(
                 out=grouped[:].bitcast(F32).rearrange("p (g r u) -> p g r u", g=PASSES, u=HALVES),
                 in_=bank[:].rearrange("p g u r -> p g r u"),
             )
             return grouped
 
+        def new_quantised():
+            codes = per_tile.tile([P, PASSES * P], U32, align_bytes=64, tag="codes")
+            scales = per_tile.tile([P, PASSES * P], U8, align_bytes=64, tag="scales")
+            return codes, scales
+
         def quantise_rows(grouped):
-            codes = per_tile.tile([P, PASSES * P], U32, align_bytes=64, bufs=O_TILES + 1)
-            scales = per_tile.tile([P, PASSES * P], U8, align_bytes=64, bufs=O_TILES + 1)
+            codes, scales = new_quantised()
             nc.vector.quantize_mx(out=codes[:].bitcast(FP8X4), scales=scales[:], in_=grouped[:])
             return codes, scales
 
@@ -117,6 +124,9 @@ def tile_visionattention_pa_s_kernel(tc, x, Wq, bq, k, out):
         for g in range(PASSES):
             q_bank = psum_q.tile([P, TILES_PER_PASS, TOKENS], F32)
             qT.append(q_bank)
+
+        x_codes = keep.tile([P, PASSES * TOKENS], U32, align_bytes=64)
+        x_scales = keep.tile([P, PASSES * TOKENS], U8, align_bytes=64)
 
         def project_tile(j, codes, scales):
             for g in range(PASSES):
@@ -133,7 +143,7 @@ def tile_visionattention_pa_s_kernel(tc, x, Wq, bq, k, out):
 
         bias = keep.tile([P, O_TILES], F32)
 
-        def finish_q_pass(g):
+        def add_bias(g):
             grouped = per_pass.tile([P, TOKENS * PACK], BF16, align_bytes=64)
             nc.vector.scalar_tensor_tensor(
                 out=grouped[:].rearrange("p (n t) -> p n t", t=PACK),
@@ -143,59 +153,100 @@ def tile_visionattention_pa_s_kernel(tc, x, Wq, bq, k, out):
                 op0=ALU.mult,
                 op1=ALU.add,
             )
+            return grouped
+
+        def quantise_q(grouped):
             codes = per_pass.tile([P, TOKENS], U32, align_bytes=64)
             scales = per_pass.tile([P, TOKENS], U8, align_bytes=64)
             nc.vector.quantize_mx(out=codes[:].bitcast(FP8X4), scales=scales[:], in_=grouped[:])
             return codes, scales
 
-        def tiles_of_round(a):
-            if 0 <= a < ROUNDS:
-                return range(a * ROUND_TILES, (a + 1) * ROUND_TILES)
-            return range(0)
-
-        banks = {}
         grouped_rows = {}
         quantised = {}
-        q_quantised = {}
-        for a in range(ROUNDS + 2):
-            for j in tiles_of_round(a):
-                banks[j] = transpose_rows(wq_words[:, j, :])
-            if a == 0:
-                bqT = psum_one.tile([P, HALVES, P], F32, tag="small")
-                for u in range(HALVES):
-                    nc.tensor.transpose(bqT[:, u, :], bq_rows[:].bitcast(F32)[:, u::HALVES], ident[:])
-                nc.vector.tensor_scalar(
-                    out=bias[:].rearrange("p (g u e) -> p g u e", g=PASSES, u=HALVES),
-                    in0=bqT[:, :, 0:PASSES].bitcast(BF16).rearrange("p u (g e) -> p g u e", e=PAIR),
-                    scalar1=1.0 / 32.0,
-                    scalar2=None,
-                    op0=ALU.mult,
-                )
-            if a == ROUNDS:
-                banks["k"] = transpose_rows(k_words)
-            for j in tiles_of_round(a - 1):
-                quantised[j] = quantise_rows(grouped_rows[j])
-            if a == ROUNDS + 1:
-                quantised["k"] = quantise_rows(grouped_rows["k"])
-            if a >= 2 and (a - 1) % ROUNDS_PER_PASS == 0:
-                g = (a - 1) // ROUNDS_PER_PASS - 1
-                q_quantised[g] = finish_q_pass(g)
-            for j in tiles_of_round(a):
-                grouped_rows[j] = empty_bank(banks[j])
-            if a == ROUNDS:
-                grouped_rows["k"] = empty_bank(banks["k"])
-            for j in tiles_of_round(a - 1):
-                project_tile(j, quantised[j][0], quantised[j][1])
+
+        def bring(j):
+            bank = transpose_rows(wq_words[:, j, :])
+            grouped_rows[j] = empty_bank(bank)
+
+        def quantise(j):
+            quantised[j] = quantise_rows(grouped_rows[j])
+
+        def project(j):
+            project_tile(j, quantised[j][0], quantised[j][1])
+
+        bring(0)
+        x_grouped = keep.tile([P, PASSES * TOKENS * PACK], BF16, align_bytes=64)
+        nc.vector.tensor_copy(
+            out=x_grouped[:].rearrange("p (g n t) -> p g n t", g=PASSES, t=PACK),
+            in_=x_sb[:].rearrange("p (g t n) -> p g n t", g=PASSES, t=PACK),
+        )
+        quantise(0)
+        nc.vector.quantize_mx(out=x_codes[:].bitcast(FP8X4), scales=x_scales[:], in_=x_grouped[:])
+        bring(1)
+        bring(2)
+        quantise(1)
+        quantise(2)
+        bring(3)
+        bring(4)
+        project(0)
+        project(1)
+        project(2)
+
+        bqT = psum_one.tile([P, HALVES, P], F32, tag="small")
+        for u in range(HALVES):
+            nc.tensor.transpose(bqT[:, u, :], bq_rows[:, u::HALVES], ident[:])
+        quantise(3)
+        nc.vector.tensor_scalar(
+            out=bias[:].rearrange("p (g u e) -> p g u e", g=PASSES, u=HALVES),
+            in0=bqT[:, :, 0:PASSES].bitcast(BF16).rearrange("p u (g e) -> p g u e", e=PAIR),
+            scalar1=1.0 / 32.0,
+            scalar2=None,
+            op0=ALU.mult,
+        )
+        quantise(4)
+        bring(5)
+        bring(6)
+        project(3)
+        project(4)
+        quantise(5)
+        q_grouped0 = add_bias(0)
+        quantise(6)
+        q0 = quantise_q(q_grouped0)
+
+        halves = []
+        for g in range(PASSES):
+            half = psum_t.tile([P, HALVES, P], F32, tag="bank")
+            transpose_pass(wq_words[:, O_TILES - 1, :], g, half)
+            halves.append(half)
+        last = new_grouped()
+        last_words = last[:].bitcast(F32).rearrange("p (g r u) -> p g r u", g=PASSES, u=HALVES)
+        nc.scalar.copy(out=last_words[:, 0, :, :], in_=halves[0][:].rearrange("p u r -> p r u"))
+        nc.vector.tensor_copy(out=last_words[:, 1, :, :], in_=halves[1][:].rearrange("p u r -> p r u"))
+        bank_k = transpose_rows(k_words)
+        project(5)
+        project(6)
+        last_codes, last_scales = new_quantised()
+        for g in range(PASSES):
+            nc.vector.quantize_mx(
+                out=last_codes[:, g * P : (g + 1) * P].bitcast(FP8X4),
+                scales=last_scales[:, g * P : (g + 1) * P],
+                in_=last[:, g * K_PASS : (g + 1) * K_PASS],
+            )
+        project_tile(O_TILES - 1, last_codes, last_scales)
+        grouped_k = empty_bank(bank_k)
+        q_grouped1 = add_bias(1)
+        k_codes, k_scales = quantise_rows(grouped_k)
+        q1 = quantise_q(q_grouped1)
 
         scores = psum_one.tile([P, TOKENS], F32, tag="small")
-        for g in range(PASSES):
+        for g, q in enumerate((q0, q1)):
             cols = slice(g * TOKENS, (g + 1) * TOKENS)
             nc.tensor.matmul_mx(
                 out=scores[:],
-                lhsT=q_quantised[g][0][:].bitcast(FP8X4),
-                lhsT_scale=q_quantised[g][1][:],
-                rhs=quantised["k"][0][:, cols].bitcast(FP8X4),
-                rhs_scale=quantised["k"][1][:, cols],
+                lhsT=q[0][:].bitcast(FP8X4),
+                lhsT_scale=q[1][:],
+                rhs=k_codes[:, cols].bitcast(FP8X4),
+                rhs_scale=k_scales[:, cols],
                 start=(g == 0),
                 stop=(g == PASSES - 1),
             )

@@ -56,17 +56,17 @@ def tile_visionattention_pa_s_kernel(tc, x, Wq, bq, k, out):
             )
 
         load_tiles(0, 1)
+        load_tiles(1, 1)
         nc.sync.dma_start(
             out=x_sb[:].rearrange("p (g tn) -> p g tn", g=PASSES),
             in_=x.rearrange("b c h w -> c (b h w)").rearrange("(g p t) n -> p g (t n)", p=P, t=PACK),
         )
-        nc.scalar.dma_start(
+        for j in range(2, 6):
+            load_tiles(j, 1)
+        nc.sync.dma_start(
             out=bq_rows[0:PASSES, :].bitcast(BF16), in_=bq.rearrange("(g w) -> g w", g=PASSES)
         )
-        load_tiles(1, 2)
-        load_tiles(3, 1)
-        load_tiles(4, 1)
-        load_tiles(5, 2)
+        load_tiles(6, 1)
         load_tiles(7, 1)
         nc.sync.dma_start(out=k_sb[:], in_=k.rearrange("b m c -> (b m) c"))
         wq_words = wq_sb[:].bitcast(F32).rearrange("p (j w) -> p j w", j=O_TILES)
@@ -100,14 +100,6 @@ def tile_visionattention_pa_s_kernel(tc, x, Wq, bq, k, out):
 
         def new_grouped():
             grouped = per_tile.tile([P, PASSES * P * PACK], BF16, align_bytes=64, tag="grouped")
-            return grouped
-
-        def empty_bank(bank):
-            grouped = new_grouped()
-            nc.scalar.copy(
-                out=grouped[:].bitcast(F32).rearrange("p (g r u) -> p g r u", g=PASSES, u=HALVES),
-                in_=bank[:].rearrange("p g u r -> p g r u"),
-            )
             return grouped
 
         def new_quantised():
@@ -161,12 +153,28 @@ def tile_visionattention_pa_s_kernel(tc, x, Wq, bq, k, out):
             nc.vector.quantize_mx(out=codes[:].bitcast(FP8X4), scales=scales[:], in_=grouped[:])
             return codes, scales
 
+        banks = {}
         grouped_rows = {}
         quantised = {}
+        LAST = O_TILES - 1
 
-        def bring(j):
-            bank = transpose_rows(wq_words[:, j, :])
-            grouped_rows[j] = empty_bank(bank)
+        def transpose(j):
+            words = k_words if j == "k" else wq_words[:, j, :]
+            if j == LAST:
+                banks[j] = []
+                for g in range(PASSES):
+                    half = psum_t.tile([P, HALVES, P], F32, tag="bank")
+                    transpose_pass(words, g, half)
+                    banks[j].append(half)
+            else:
+                banks[j] = transpose_rows(words)
+
+        def empty(j, copy):
+            grouped_rows[j] = new_grouped()
+            copy(
+                out=grouped_rows[j][:].bitcast(F32).rearrange("p (g r u) -> p g r u", g=PASSES, u=HALVES),
+                in_=banks[j][:].rearrange("p g u r -> p g r u"),
+            )
 
         def quantise(j):
             quantised[j] = quantise_rows(grouped_rows[j])
@@ -174,7 +182,10 @@ def tile_visionattention_pa_s_kernel(tc, x, Wq, bq, k, out):
         def project(j):
             project_tile(j, quantised[j][0], quantised[j][1])
 
-        bring(0)
+        transpose(0)
+        empty(0, nc.scalar.copy)
+        transpose(1)
+        empty(1, nc.scalar.copy)
         x_grouped = keep.tile([P, PASSES * TOKENS * PACK], BF16, align_bytes=64)
         nc.vector.tensor_copy(
             out=x_grouped[:].rearrange("p (g n t) -> p g n t", g=PASSES, t=PACK),
@@ -182,20 +193,23 @@ def tile_visionattention_pa_s_kernel(tc, x, Wq, bq, k, out):
         )
         quantise(0)
         nc.vector.quantize_mx(out=x_codes[:].bitcast(FP8X4), scales=x_scales[:], in_=x_grouped[:])
-        bring(1)
-        bring(2)
         quantise(1)
-        quantise(2)
-        bring(3)
-        bring(4)
+        transpose(2)
+        empty(2, nc.scalar.copy)
+        transpose(3)
+        empty(3, nc.vector.tensor_copy)
+        transpose(4)
+        empty(4, nc.scalar.copy)
         project(0)
         project(1)
-        project(2)
+        quantise(2)
+        quantise(3)
+        transpose(5)
+        empty(5, nc.scalar.copy)
 
         bqT = psum_one.tile([P, HALVES, P], F32, tag="small")
         for u in range(HALVES):
             nc.tensor.transpose(bqT[:, u, :], bq_rows[:, u::HALVES], ident[:])
-        quantise(3)
         nc.vector.tensor_scalar(
             out=bias[:].rearrange("p (g u e) -> p g u e", g=PASSES, u=HALVES),
             in0=bqT[:, :, 0:PASSES].bitcast(BF16).rearrange("p u (g e) -> p g u e", e=PAIR),
@@ -203,27 +217,24 @@ def tile_visionattention_pa_s_kernel(tc, x, Wq, bq, k, out):
             scalar2=None,
             op0=ALU.mult,
         )
-        quantise(4)
-        bring(5)
-        bring(6)
+        project(2)
         project(3)
-        project(4)
-        quantise(5)
+        quantise(4)
         q_grouped0 = add_bias(0)
-        quantise(6)
-        q0 = quantise_q(q_grouped0)
+        transpose(6)
+        empty(6, nc.scalar.copy)
+        quantise(5)
 
-        halves = []
-        for g in range(PASSES):
-            half = psum_t.tile([P, HALVES, P], F32, tag="bank")
-            transpose_pass(wq_words[:, O_TILES - 1, :], g, half)
-            halves.append(half)
+        transpose(LAST)
         last = new_grouped()
         last_words = last[:].bitcast(F32).rearrange("p (g r u) -> p g r u", g=PASSES, u=HALVES)
-        nc.scalar.copy(out=last_words[:, 0, :, :], in_=halves[0][:].rearrange("p u r -> p r u"))
-        nc.vector.tensor_copy(out=last_words[:, 1, :, :], in_=halves[1][:].rearrange("p u r -> p r u"))
-        bank_k = transpose_rows(k_words)
+        nc.scalar.copy(out=last_words[:, 0, :, :], in_=banks[LAST][0][:].rearrange("p u r -> p r u"))
+        nc.vector.tensor_copy(out=last_words[:, 1, :, :], in_=banks[LAST][1][:].rearrange("p u r -> p r u"))
+        project(4)
+        transpose("k")
+        empty("k", nc.scalar.copy)
         project(5)
+        quantise(6)
         project(6)
         last_codes, last_scales = new_quantised()
         for g in range(PASSES):
@@ -232,10 +243,11 @@ def tile_visionattention_pa_s_kernel(tc, x, Wq, bq, k, out):
                 scales=last_scales[:, g * P : (g + 1) * P],
                 in_=last[:, g * K_PASS : (g + 1) * K_PASS],
             )
-        project_tile(O_TILES - 1, last_codes, last_scales)
-        grouped_k = empty_bank(bank_k)
+        project_tile(LAST, last_codes, last_scales)
+        q0 = quantise_q(q_grouped0)
+        quantise("k")
+        k_codes, k_scales = quantised["k"]
         q_grouped1 = add_bias(1)
-        k_codes, k_scales = quantise_rows(grouped_k)
         q1 = quantise_q(q_grouped1)
 
         scores = psum_one.tile([P, TOKENS], F32, tag="small")

@@ -40,8 +40,7 @@ def tile_visionattention_pa_s_kernel(tc, x, Wq, bq, k, out):
 
         zero_col = keep.tile([P, 1], F32)
         nc.vector.memset(zero_col[:], 0.0)
-        bq_rows = keep.tile([P, K_PASS // PAIR], F32)
-        nc.vector.memset(bq_rows[:], 0.0)
+        bq_sb = keep.tile([P, O_TILES], BF16)
 
         wq_sb = keep.tile([P, O_TILES * CHANNELS], BF16)
         wq_tiles = wq_sb[:].rearrange("p (j c) -> p j c", j=O_TILES)
@@ -61,14 +60,14 @@ def tile_visionattention_pa_s_kernel(tc, x, Wq, bq, k, out):
             out=x_sb[:].rearrange("p (g tn) -> p g tn", g=PASSES),
             in_=x.rearrange("b c h w -> c (b h w)").rearrange("(g p t) n -> p g (t n)", p=P, t=PACK),
         )
-        for j in range(2, 6):
+        for j in range(2, O_TILES - 1):
             load_tiles(j, 1)
-        nc.sync.dma_start(
-            out=bq_rows[0:PASSES, :].bitcast(BF16), in_=bq.rearrange("(g w) -> g w", g=PASSES)
-        )
-        load_tiles(6, 1)
-        load_tiles(7, 1)
         nc.sync.dma_start(out=k_sb[:], in_=k.rearrange("b m c -> (b m) c"))
+        load_tiles(O_TILES - 1, 1)
+        nc.sync.dma_start(
+            out=bq_sb[:].rearrange("p (g t) -> p g t", g=PASSES),
+            in_=bq.rearrange("(g p t) -> p g t", p=P, t=PACK),
+        )
         wq_words = wq_sb[:].bitcast(F32).rearrange("p (j w) -> p j w", j=O_TILES)
         k_words = k_sb[:].bitcast(F32)
 
@@ -134,6 +133,9 @@ def tile_visionattention_pa_s_kernel(tc, x, Wq, bq, k, out):
                 )
 
         bias = keep.tile([P, O_TILES], F32)
+        nc.gpsimd.tensor_scalar(
+            out=bias[:], in0=bq_sb[:], scalar1=1.0 / 32.0, scalar2=None, op0=ALU.mult
+        )
 
         def add_bias(g):
             grouped = per_pass.tile([P, TOKENS * PACK], BF16, align_bytes=64)
@@ -182,60 +184,31 @@ def tile_visionattention_pa_s_kernel(tc, x, Wq, bq, k, out):
         def project(j):
             project_tile(j, quantised[j][0], quantised[j][1])
 
-        transpose(0)
-        empty(0, nc.scalar.copy)
-        transpose(1)
-        empty(1, nc.scalar.copy)
-        x_grouped = keep.tile([P, PASSES * TOKENS * PACK], BF16, align_bytes=64)
-        nc.vector.tensor_copy(
-            out=x_grouped[:].rearrange("p (g n t) -> p g n t", g=PASSES, t=PACK),
-            in_=x_sb[:].rearrange("p (g t n) -> p g n t", g=PASSES, t=PACK),
-        )
-        quantise(0)
-        nc.vector.quantize_mx(out=x_codes[:].bitcast(FP8X4), scales=x_scales[:], in_=x_grouped[:])
-        quantise(1)
-        transpose(2)
-        empty(2, nc.scalar.copy)
-        transpose(3)
-        empty(3, nc.vector.tensor_copy)
-        transpose(4)
-        empty(4, nc.scalar.copy)
-        project(0)
-        project(1)
-        quantise(2)
-        quantise(3)
-        transpose(5)
-        empty(5, nc.scalar.copy)
+        order = list(range(LAST)) + ["k", LAST]
+        for j in order:
+            transpose(j)
+            if j != LAST:
+                empty(j, nc.scalar.copy)
+            if j == 0:
+                quantise(0)
+                x_grouped = keep.tile([P, PASSES * TOKENS * PACK], BF16, align_bytes=64)
+                nc.vector.tensor_copy(
+                    out=x_grouped[:].rearrange("p (g n t) -> p g n t", g=PASSES, t=PACK),
+                    in_=x_sb[:].rearrange("p (g t n) -> p g n t", g=PASSES, t=PACK),
+                )
+            elif j == 1:
+                quantise(1)
+                nc.vector.quantize_mx(
+                    out=x_codes[:].bitcast(FP8X4), scales=x_scales[:], in_=x_grouped[:]
+                )
+            elif j in range(LAST):
+                quantise(j)
 
-        bqT = psum_one.tile([P, HALVES, P], F32, tag="small")
-        for u in range(HALVES):
-            nc.tensor.transpose(bqT[:, u, :], bq_rows[:, u::HALVES], ident[:])
-        nc.vector.tensor_scalar(
-            out=bias[:].rearrange("p (g u e) -> p g u e", g=PASSES, u=HALVES),
-            in0=bqT[:, :, 0:PASSES].bitcast(BF16).rearrange("p u (g e) -> p g u e", e=PAIR),
-            scalar1=1.0 / 32.0,
-            scalar2=None,
-            op0=ALU.mult,
-        )
-        project(2)
-        project(3)
-        quantise(4)
-        q_grouped0 = add_bias(0)
-        transpose(6)
-        empty(6, nc.scalar.copy)
-        quantise(5)
-
-        transpose(LAST)
         last = new_grouped()
         last_words = last[:].bitcast(F32).rearrange("p (g r u) -> p g r u", g=PASSES, u=HALVES)
         nc.scalar.copy(out=last_words[:, 0, :, :], in_=banks[LAST][0][:].rearrange("p u r -> p r u"))
         nc.vector.tensor_copy(out=last_words[:, 1, :, :], in_=banks[LAST][1][:].rearrange("p u r -> p r u"))
-        project(4)
-        transpose("k")
-        empty("k", nc.scalar.copy)
-        project(5)
-        quantise(6)
-        project(6)
+        quantise("k")
         last_codes, last_scales = new_quantised()
         for g in range(PASSES):
             nc.vector.quantize_mx(
@@ -243,11 +216,13 @@ def tile_visionattention_pa_s_kernel(tc, x, Wq, bq, k, out):
                 scales=last_scales[:, g * P : (g + 1) * P],
                 in_=last[:, g * K_PASS : (g + 1) * K_PASS],
             )
-        project_tile(LAST, last_codes, last_scales)
-        q0 = quantise_q(q_grouped0)
-        quantise("k")
+        quantised[LAST] = (last_codes, last_scales)
+        for j in range(O_TILES):
+            project(j)
         k_codes, k_scales = quantised["k"]
+        q_grouped0 = add_bias(0)
         q_grouped1 = add_bias(1)
+        q0 = quantise_q(q_grouped0)
         q1 = quantise_q(q_grouped1)
 
         scores = psum_one.tile([P, TOKENS], F32, tag="small")

@@ -23,6 +23,7 @@ HALVES = PACK // PAIR
 O_TILES = CHANNELS // P
 TILES_PER_PASS = O_TILES // PASSES
 WARM_COLUMNS = 512
+HOLD_COLUMNS = 160
 
 FLOPS = 2 * TOKENS * CHANNELS * CHANNELS + 2 * TOKENS * TOKENS * CHANNELS
 
@@ -72,13 +73,17 @@ def tile_visionattention_pa_s_kernel(tc, x, Wq, bq, k, out):
         k_words = k_sb[:].bitcast(F32)
 
         warm_bank = psum_one.tile([P, WARM_COLUMNS], F32, tag="small")
-        nc.tensor.matmul(
-            warm_bank[:],
-            lhsT=zero_col[:].to_broadcast([P, P]),
-            rhs=zero_col[:].to_broadcast([P, WARM_COLUMNS]),
-            start=True,
-            stop=True,
-        )
+
+        def warm_tensor(columns):
+            nc.tensor.matmul(
+                warm_bank[:, 0:columns],
+                lhsT=zero_col[:].to_broadcast([P, P]),
+                rhs=zero_col[:].to_broadcast([P, columns]),
+                start=True,
+                stop=True,
+            )
+
+        warm_tensor(WARM_COLUMNS)
 
         ident = keep.tile([P, P], F32)
         make_identity(nc, ident[:])
@@ -187,6 +192,8 @@ def tile_visionattention_pa_s_kernel(tc, x, Wq, bq, k, out):
         order = list(range(LAST)) + ["k", LAST]
         for j in order:
             transpose(j)
+            if j in (2, 5):
+                warm_tensor(HOLD_COLUMNS)
             if j != LAST:
                 empty(j, nc.scalar.copy)
             if j == 0:

@@ -23,7 +23,7 @@ HALVES = PACK // PAIR
 O_TILES = CHANNELS // P
 TILES_PER_PASS = O_TILES // PASSES
 WARM_COLUMNS = 512
-HOLD_COLUMNS = 160
+HOLD_COLUMNS = {2: 160, 6: 200}
 
 FLOPS = 2 * TOKENS * CHANNELS * CHANNELS + 2 * TOKENS * TOKENS * CHANNELS
 
@@ -56,13 +56,12 @@ def tile_visionattention_pa_s_kernel(tc, x, Wq, bq, k, out):
             )
 
         load_tiles(0, 1)
-        load_tiles(1, 1)
+        for j in range(1, O_TILES - 1):
+            load_tiles(j, 1)
         nc.sync.dma_start(
             out=x_sb[:].rearrange("p (g tn) -> p g tn", g=PASSES),
             in_=x.rearrange("b c h w -> c (b h w)").rearrange("(g p t) n -> p g (t n)", p=P, t=PACK),
         )
-        for j in range(2, O_TILES - 1):
-            load_tiles(j, 1)
         nc.sync.dma_start(out=k_sb[:], in_=k.rearrange("b m c -> (b m) c"))
         load_tiles(O_TILES - 1, 1)
         nc.sync.dma_start(
@@ -192,24 +191,22 @@ def tile_visionattention_pa_s_kernel(tc, x, Wq, bq, k, out):
         order = list(range(LAST)) + ["k", LAST]
         for j in order:
             transpose(j)
-            if j in (2, 5):
-                warm_tensor(HOLD_COLUMNS)
+            if j in HOLD_COLUMNS:
+                warm_tensor(HOLD_COLUMNS[j])
             if j != LAST:
                 empty(j, nc.scalar.copy)
-            if j == 0:
-                quantise(0)
+            if j in range(LAST):
+                quantise(j)
+            if j == 4:
                 x_grouped = keep.tile([P, PASSES * TOKENS * PACK], BF16, align_bytes=64)
                 nc.vector.tensor_copy(
                     out=x_grouped[:].rearrange("p (g n t) -> p g n t", g=PASSES, t=PACK),
                     in_=x_sb[:].rearrange("p (g t n) -> p g n t", g=PASSES, t=PACK),
                 )
-            elif j == 1:
-                quantise(1)
+            elif j == 5:
                 nc.vector.quantize_mx(
                     out=x_codes[:].bitcast(FP8X4), scales=x_scales[:], in_=x_grouped[:]
                 )
-            elif j in range(LAST):
-                quantise(j)
 
         last = new_grouped()
         last_words = last[:].bitcast(F32).rearrange("p (g r u) -> p g r u", g=PASSES, u=HALVES)

@@ -166,7 +166,7 @@ def tile_visionattention_pa_s_kernel(tc, x, Wq, bq, k, out):
 
         def transpose(j):
             words = k_words if j == "k" else wq_words[:, j, :]
-            if j == LAST:
+            if j in ("k", LAST):
                 banks[j] = []
                 for g in range(PASSES):
                     half = psum_t.tile([P, HALVES, P], F32, tag="bank")
@@ -189,11 +189,12 @@ def tile_visionattention_pa_s_kernel(tc, x, Wq, bq, k, out):
             project_tile(j, quantised[j][0], quantised[j][1])
 
         order = list(range(LAST)) + ["k", LAST]
+        split = ("k", LAST)
         for j in order:
             transpose(j)
             if j in HOLD_COLUMNS:
                 warm_tensor(HOLD_COLUMNS[j])
-            if j != LAST:
+            if j not in split:
                 empty(j, nc.scalar.copy)
             if j in range(LAST):
                 quantise(j)
@@ -208,19 +209,32 @@ def tile_visionattention_pa_s_kernel(tc, x, Wq, bq, k, out):
                     out=x_codes[:].bitcast(FP8X4), scales=x_scales[:], in_=x_grouped[:]
                 )
 
-        last = new_grouped()
-        last_words = last[:].bitcast(F32).rearrange("p (g r u) -> p g r u", g=PASSES, u=HALVES)
-        nc.scalar.copy(out=last_words[:, 0, :, :], in_=banks[LAST][0][:].rearrange("p u r -> p r u"))
-        nc.vector.tensor_copy(out=last_words[:, 1, :, :], in_=banks[LAST][1][:].rearrange("p u r -> p r u"))
-        quantise("k")
-        last_codes, last_scales = new_quantised()
-        for g in range(PASSES):
-            nc.vector.quantize_mx(
-                out=last_codes[:, g * P : (g + 1) * P].bitcast(FP8X4),
-                scales=last_scales[:, g * P : (g + 1) * P],
-                in_=last[:, g * K_PASS : (g + 1) * K_PASS],
+        def empty_pass(j, g, copy):
+            copy(
+                out=grouped_rows[j][:].bitcast(F32).rearrange(
+                    "p (g r u) -> p g r u", g=PASSES, u=HALVES
+                )[:, g, :, :],
+                in_=banks[j][g][:].rearrange("p u r -> p r u"),
             )
-        quantised[LAST] = (last_codes, last_scales)
+
+        def quantise_pass(j, g):
+            codes, scales = quantised[j]
+            nc.vector.quantize_mx(
+                out=codes[:, g * P : (g + 1) * P].bitcast(FP8X4),
+                scales=scales[:, g * P : (g + 1) * P],
+                in_=grouped_rows[j][:, g * K_PASS : (g + 1) * K_PASS],
+            )
+
+        for j in split:
+            grouped_rows[j] = new_grouped()
+            quantised[j] = new_quantised()
+        empty_pass("k", 0, nc.scalar.copy)
+        empty_pass("k", 1, nc.vector.tensor_copy)
+        empty_pass(LAST, 0, nc.scalar.copy)
+        empty_pass(LAST, 1, nc.scalar.copy)
+        for j in split:
+            for g in range(PASSES):
+                quantise_pass(j, g)
         for j in range(O_TILES):
             project(j)
         k_codes, k_scales = quantised["k"]

from contextlib import ExitStack

import concourse.mybir as mybir
from concourse.masks import make_identity

F32 = mybir.dt.float32
BF16 = mybir.dt.bfloat16
U32 = mybir.dt.uint32
U8 = mybir.dt.uint8
FP8X4 = mybir.dt.float8_e4m3fn_x4
ACT = mybir.ActivationFunctionType
ALU = mybir.AluOpType
AXIS = mybir.AxisListType

P = 128
TOKENS = 128
CHANNELS = 1024
PACK = 4
K_PASS = P * PACK
PASSES = CHANNELS // K_PASS
PAIR = 2
HALVES = PACK // PAIR
O_TILES = CHANNELS // P
TILES_PER_PASS = O_TILES // PASSES
WARM_COLUMNS = 512
HOLD_COLUMNS = {2: 160, 6: 200}

FLOPS = 2 * TOKENS * CHANNELS * CHANNELS + 2 * TOKENS * TOKENS * CHANNELS


def tile_visionattention_pa_s_kernel(tc, x, Wq, bq, k, out):
    nc = tc.nc
    with ExitStack() as ctx:
        ctx.enter_context(tc.manual_schedule())
        keep = ctx.enter_context(tc.tile_pool(name="keep", bufs=1))
        per_tile = ctx.enter_context(tc.tile_pool(name="per_tile", bufs=O_TILES + 1))
        per_pass = ctx.enter_context(tc.tile_pool(name="per_pass", bufs=PASSES))
        psum_t = ctx.enter_context(tc.psum_pool(name="psum_t", bufs=5))
        psum_q = ctx.enter_context(tc.psum_pool(name="psum_q", bufs=PASSES))
        psum_one = ctx.enter_context(tc.psum_pool(name="psum_one", bufs=1))

        zero_col = keep.tile([P, 1], F32)
        nc.vector.memset(zero_col[:], 0.0)
        bq_sb = keep.tile([P, O_TILES], BF16)

        wq_sb = keep.tile([P, O_TILES * CHANNELS], BF16)
        wq_tiles = wq_sb[:].rearrange("p (j c) -> p j c", j=O_TILES)
        wq_rows = Wq.rearrange("(g r t) c -> r g t c", r=P, t=PACK)
        x_sb = keep.tile([P, CHANNELS], BF16)
        k_sb = keep.tile([P, CHANNELS], BF16)

        def load_tiles(first, count):
            nc.sync.dma_start(
                out=wq_tiles[:, first : first + count, :],
                in_=wq_rows[:, first // PACK, first % PACK : first % PACK + count, :],
            )

        load_tiles(0, 1)
        for j in range(1, O_TILES - 1):
            load_tiles(j, 1)
        nc.sync.dma_start(
            out=x_sb[:].rearrange("p (g tn) -> p g tn", g=PASSES),
            in_=x.rearrange("b c h w -> c (b h w)").rearrange("(g p t) n -> p g (t n)", p=P, t=PACK),
        )
        nc.sync.dma_start(out=k_sb[:], in_=k.rearrange("b m c -> (b m) c"))
        load_tiles(O_TILES - 1, 1)
        nc.sync.dma_start(
            out=bq_sb[:].rearrange("p (g t) -> p g t", g=PASSES),
            in_=bq.rearrange("(g p t) -> p g t", p=P, t=PACK),
        )
        wq_words = wq_sb[:].bitcast(F32).rearrange("p (j w) -> p j w", j=O_TILES)
        k_words = k_sb[:].bitcast(F32)

        warm_bank = psum_one.tile([P, WARM_COLUMNS], F32, tag="small")

        def warm_tensor(columns):
            nc.tensor.matmul(
                warm_bank[:, 0:columns],
                lhsT=zero_col[:].to_broadcast([P, P]),
                rhs=zero_col[:].to_broadcast([P, columns]),
                start=True,
                stop=True,
            )

        warm_tensor(WARM_COLUMNS)

        ident = keep.tile([P, P], F32)
        make_identity(nc, ident[:])

        warm = keep.tile([P, 1], F32)
        nc.scalar.activation(out=warm[:], in_=zero_col[:], func=ACT.Exp)

        def transpose_pass(words, g, bank):
            for u in range(HALVES):
                group = slice(g * HALVES * P + u, (g + 1) * HALVES * P, HALVES)
                nc.tensor.transpose(bank[:, u, :], words[:, group], ident[:])

        def transpose_rows(words):
            bank = psum_t.tile([P, PASSES, HALVES, P], F32, tag="bank")
            for g in range(PASSES):
                transpose_pass(words, g, bank[:, g, :, :])
            return bank

        def new_grouped():
            grouped = per_tile.tile([P, PASSES * P * PACK], BF16, align_bytes=64, tag="grouped")
            return grouped

        def new_quantised():
            codes = per_tile.tile([P, PASSES * P], U32, align_bytes=64, tag="codes")
            scales = per_tile.tile([P, PASSES * P], U8, align_bytes=64, tag="scales")
            return codes, scales

        def quantise_rows(grouped):
            codes, scales = new_quantised()
            nc.vector.quantize_mx(out=codes[:].bitcast(FP8X4), scales=scales[:], in_=grouped[:])
            return codes, scales

        qT = []
        for g in range(PASSES):
            q_bank = psum_q.tile([P, TILES_PER_PASS, TOKENS], F32)
            qT.append(q_bank)

        x_codes = keep.tile([P, PASSES * TOKENS], U32, align_bytes=64)
        x_scales = keep.tile([P, PASSES * TOKENS], U8, align_bytes=64)

        def project_tile(j, codes, scales):
            for g in range(PASSES):
                cols = slice(g * P, (g + 1) * P)
                nc.tensor.matmul_mx(
                    out=qT[j // TILES_PER_PASS][:, j % TILES_PER_PASS, :],
                    lhsT=codes[:, cols].bitcast(FP8X4),
                    lhsT_scale=scales[:, cols],
                    rhs=x_codes[:, cols].bitcast(FP8X4),
                    rhs_scale=x_scales[:, cols],
                    start=(g == 0),
                    stop=(g == PASSES - 1),
                )

        bias = keep.tile([P, O_TILES], F32)
        nc.gpsimd.tensor_scalar(
            out=bias[:], in0=bq_sb[:], scalar1=1.0 / 32.0, scalar2=None, op0=ALU.mult
        )

        def add_bias(g):
            grouped = per_pass.tile([P, TOKENS * PACK], BF16, align_bytes=64)
            nc.vector.scalar_tensor_tensor(
                out=grouped[:].rearrange("p (n t) -> p n t", t=PACK),
                in0=qT[g][:].rearrange("p t n -> p n t"),
                scalar=1.0 / 32.0,
                in1=bias[:, g * PACK : (g + 1) * PACK].unsqueeze(1).to_broadcast([P, TOKENS, PACK]),
                op0=ALU.mult,
                op1=ALU.add,
            )
            return grouped

        def quantise_q(grouped):
            codes = per_pass.tile([P, TOKENS], U32, align_bytes=64)
            scales = per_pass.tile([P, TOKENS], U8, align_bytes=64)
            nc.vector.quantize_mx(out=codes[:].bitcast(FP8X4), scales=scales[:], in_=grouped[:])
            return codes, scales

        banks = {}
        grouped_rows = {}
        quantised = {}
        LAST = O_TILES - 1

        def transpose(j):
            words = k_words if j == "k" else wq_words[:, j, :]
            if j in ("k", LAST):
                banks[j] = []
                for g in range(PASSES):
                    half = psum_t.tile([P, HALVES, P], F32, tag="bank")
                    transpose_pass(words, g, half)
                    banks[j].append(half)
            else:
                banks[j] = transpose_rows(words)

        def empty(j, copy):
            grouped_rows[j] = new_grouped()
            copy(
                out=grouped_rows[j][:].bitcast(F32).rearrange("p (g r u) -> p g r u", g=PASSES, u=HALVES),
                in_=banks[j][:].rearrange("p g u r -> p g r u"),
            )

        def quantise(j):
            quantised[j] = quantise_rows(grouped_rows[j])

        def project(j):
            project_tile(j, quantised[j][0], quantised[j][1])

        order = list(range(LAST)) + ["k", LAST]
        split = ("k", LAST)
        for j in order:
            transpose(j)
            if j in HOLD_COLUMNS:
                warm_tensor(HOLD_COLUMNS[j])
            if j not in split:
                empty(j, nc.scalar.copy)
            if j in range(LAST):
                quantise(j)
            if j == 4:
                x_grouped = keep.tile([P, PASSES * TOKENS * PACK], BF16, align_bytes=64)
                nc.vector.tensor_copy(
                    out=x_grouped[:].rearrange("p (g n t) -> p g n t", g=PASSES, t=PACK),
                    in_=x_sb[:].rearrange("p (g t n) -> p g n t", g=PASSES, t=PACK),
                )
            elif j == 5:
                nc.vector.quantize_mx(
                    out=x_codes[:].bitcast(FP8X4), scales=x_scales[:], in_=x_grouped[:]
                )

        def empty_pass(j, g, copy):
            copy(
                out=grouped_rows[j][:].bitcast(F32).rearrange(
                    "p (g r u) -> p g r u", g=PASSES, u=HALVES
                )[:, g, :, :],
                in_=banks[j][g][:].rearrange("p u r -> p r u"),
            )

        def quantise_pass(j, g):
            codes, scales = quantised[j]
            nc.vector.quantize_mx(
                out=codes[:, g * P : (g + 1) * P].bitcast(FP8X4),
                scales=scales[:, g * P : (g + 1) * P],
                in_=grouped_rows[j][:, g * K_PASS : (g + 1) * K_PASS],
            )

        for j in split:
            grouped_rows[j] = new_grouped()
            quantised[j] = new_quantised()
        empty_pass("k", 0, nc.scalar.copy)
        empty_pass("k", 1, nc.vector.tensor_copy)
        empty_pass(LAST, 0, nc.scalar.copy)
        empty_pass(LAST, 1, nc.scalar.copy)
        for j in split:
            for g in range(PASSES):
                quantise_pass(j, g)
        for j in range(O_TILES):
            project(j)
        k_codes, k_scales = quantised["k"]
        q_grouped0 = add_bias(0)
        q_grouped1 = add_bias(1)
        q0 = quantise_q(q_grouped0)
        q1 = quantise_q(q_grouped1)

        scores = psum_one.tile([P, TOKENS], F32, tag="small")
        for g, q in enumerate((q0, q1)):
            cols = slice(g * TOKENS, (g + 1) * TOKENS)
            nc.tensor.matmul_mx(
                out=scores[:],
                lhsT=q[0][:].bitcast(FP8X4),
                lhsT_scale=q[1][:],
                rhs=k_codes[:, cols].bitcast(FP8X4),
                rhs_scale=k_scales[:, cols],
                start=(g == 0),
                stop=(g == PASSES - 1),
            )

        neg_max = keep.tile([P, 1], F32)
        nc.vector.tensor_reduce(out=neg_max[:], in_=scores[:], axis=AXIS.X, op=ALU.max, negate=True)
        expo = keep.tile([P, TOKENS], F32)
        row_sum = keep.tile([P, 1], F32)
        nc.scalar.activation(
            out=expo[:], in_=scores[:], func=ACT.Exp, bias=neg_max[:], scale=1.0, accum_out=row_sum[:]
        )
        inv_sum = keep.tile([P, 1], F32)
        nc.vector.reciprocal(out=inv_sum[:], in_=row_sum[:])
        prob = keep.tile([P, TOKENS], F32)
        nc.vector.tensor_scalar(
            out=prob[:], in0=expo[:], scalar1=inv_sum[:, 0:1], scalar2=None, op0=ALU.mult
        )
        nc.sync.dma_start(out=out.rearrange("b n m -> (b n) m"), in_=prob[:])
